import numpy as np
import ml_dtypes


def mxq(x, axis, fmt="e4m3"):
    dtype, down = {"e4m3": (ml_dtypes.float8_e4m3fn, 7), "e5m2": (ml_dtypes.float8_e5m2, 14)}[fmt]
    v = np.moveaxis(np.asarray(x, np.float32).astype(ml_dtypes.bfloat16).astype(np.float64), axis, -1)
    blocks = v.reshape(v.shape[:-1] + (-1, 32))
    amax = np.abs(blocks).max(-1, keepdims=True)
    byte = np.maximum(np.where(amax > 0, np.frexp(amax)[1] - 1 + 127, 0) - down, 1)
    scale = np.exp2(byte - 127.0)
    codes = (blocks / scale).astype(np.float32).astype(dtype).astype(np.float64)
    return np.moveaxis((codes * scale).reshape(v.shape), -1, axis)


WIDE = False


def mx_kscale(k):
    if not WIDE:
        return np.ones(k)
    levels = np.array([10, -10, 5, -5, 0])
    a = np.random.permutation(np.resize(levels, k // 512 * 4)).reshape(k // 512, 4)
    idx = np.arange(k)
    return np.exp2(a[idx // 512, idx % 128 // 32])


BF16 = ml_dtypes.bfloat16


def bf(x):
    return np.asarray(x, np.float32).astype(BF16)


def f64(x):
    return np.asarray(x).astype(np.float64)


B, NH, NW, C, K, P = 2, 8, 8, 512, 1024, 4
T = P * P
HAD = np.array([[1.0, 1.0, 1.0, 1.0],
                [1.0, -1.0, 1.0, -1.0],
                [1.0, 1.0, -1.0, -1.0],
                [1.0, -1.0, -1.0, 1.0]])


def setup_inputs():
    s = mx_kscale(C)
    return {"trans": bf(np.random.standard_normal((T, B, NH, NW, C)) * s),
            "weight": bf(np.random.standard_normal((T, C, K)) * 0.5 * P / np.sqrt(C) / s[:, None]),
            "bias": bf(np.random.standard_normal((1, 1, 1, K)) * 0.2)}


def reference(trans, weight, bias):
    x = f64(trans).reshape(T, B * NH * NW, C)
    y = mxq(x, 2, "e4m3") @ mxq(f64(weight), 1, "e4m3")
    y = y.reshape(P, P, B, NH, NW, K)
    r = np.stack([sum(HAD[p, u] * y[u] for u in range(P)) for p in range(P)])
    z = np.stack([sum(HAD[q, v] * r[:, v] for v in range(P)) for q in range(P)], axis=1) / T
    z = z.transpose(2, 3, 0, 4, 1, 5)
    return z.reshape(B, P * NH, P * NW, K) + f64(bias)

@@ -1,0 +1,209 @@
+from contextlib import ExitStack
+
+import concourse.bass as bass
+import concourse.mybir as mybir
+import concourse.tile as tile
+from concourse.masks import make_identity
+
+F32 = mybir.dt.float32
+BF16 = mybir.dt.bfloat16
+U32 = mybir.dt.uint32
+U8 = mybir.dt.uint8
+FP8X4 = mybir.dt.float8_e4m3fn_x4
+ALU = mybir.AluOpType
+
+P = 128
+T = 16
+C = 512
+K = 1024
+FLOPS = 2 * T * P * C * K
+
+CHUNKS = [(0, 512), (512, 512)]
+MODE8 = [True, True]
+V_REGROUP = (3, 7, 19, 23)
+RAW_BUFS = 6
+GRP_BUFS = 4
+CODE_BUFS = 10
+SCALE = 1.0 / 16.0
+
+
+def sign_neg(a, b):
+    x = a & b
+    return ((x & 1) + ((x >> 1) & 1)) % 2 == 1
+
+
+def tile_iwht3layer_pa_kernel(tc, trans, weight, bias, out):
+    nc = tc.nc
+    with ExitStack() as ctx:
+        const = ctx.enter_context(tc.tile_pool(name="const", bufs=1))
+        xpool = ctx.enter_context(tc.tile_pool(name="xpool", bufs=1))
+        wpool = ctx.enter_context(tc.tile_pool(name="wpool", bufs=2))
+        hpool = ctx.enter_context(tc.tile_pool(name="hpool", bufs=2))
+        psum = ctx.enter_context(tc.psum_pool(name="psum", bufs=1))
+
+        ident = const.tile([P, P], F32, name="ident")
+        make_identity(nc, ident[:])
+        bias_bc = const.tile([P, K], BF16, name="bias_bc")
+        nc.gpsimd.dma_start(
+            out=bias_bc[:],
+            in_=bias.rearrange("a b c k -> (a b c k)").partition_broadcast(P),
+        )
+
+        x_view = trans.rearrange("(u v) b i j c -> v (b i j) u c", v=4)
+        w_view = weight.rearrange("t (p j) k -> t p j k", j=4)
+        out_view = out.rearrange("b (i p) (j q) k -> p q (b i) j k", p=4, q=4)
+
+        def bank(b, name):
+            return psum.tile([P, 512], F32, tag="bank%d" % b, name=name)
+
+        items = []
+        for ch in range(len(CHUNKS)):
+            for v in range(4):
+                for u in range(4):
+                    items.append((ch, v, u))
+
+        raws = {}
+
+        def load_w(idx):
+            ch, v, u = items[idx]
+            k0, n = CHUNKS[ch]
+            raw = wpool.tile([P, 4, n], BF16, tag="raw", bufs=RAW_BUFS, name="raw%d" % idx)
+            nc.sync.dma_start(out=raw[:], in_=w_view[4 * u + v][:, :, k0 : k0 + n])
+            raws[idx] = raw
+
+        xraw = {}
+
+        def load_x(v):
+            xr = xpool.tile([P, 4 * C], BF16, name="xraw%d" % v)
+            nc.sync.dma_start(out=xr[:].rearrange("p (u c) -> p u c", u=4), in_=x_view[v])
+            xraw[v] = xr
+
+        for v in range(4):
+            load_x(v)
+            load_w(v)
+
+        xc = {}
+        xs = {}
+        for v in range(4):
+            xw = xraw[v][:].bitcast(F32).rearrange("p (u w h) -> p u h w", u=4, h=2)
+            xpm = xpool.tile([P, 2 * 4 * P * 4], BF16, tag="xpm", bufs=2, name="xpm%d" % v, align_bytes=64)
+            xpm_w = xpm[:].bitcast(F32).rearrange("p (s u m h) -> p s u m h", s=2, u=4, h=2)
+            for g in range(2):
+                xt = bank(2 * v + g, "xt%d_%d" % (v, g))
+                xt4 = xt[:].rearrange("p (u h m) -> p u h m", u=2, h=2)
+                for u2 in range(2):
+                    for h in range(2):
+                        nc.tensor.transpose(xt4[:, u2, h, :], xw[:, 2 * g + u2, h, :], ident[:])
+                src = xt[:].rearrange("p (u h m) -> p u m h", u=2, h=2)
+                dst = xpm_w[:, 0, 2 * g : 2 * g + 2, :, :]
+                if g == 0:
+                    nc.scalar.copy(out=dst, in_=src)
+                else:
+                    nc.vector.tensor_copy(out=dst, in_=src)
+            half = 4 * P * 4
+            nc.vector.tensor_scalar_mul(out=xpm[:, half : 2 * half], in0=xpm[:, 0:half], scalar1=-1.0)
+            xcv = xpool.tile([P, 2 * 4 * P], U32, name="xc%d" % v, align_bytes=64)
+            xsv = xpool.tile([P, 2 * 4 * P], U8, name="xs%d" % v, align_bytes=64)
+            nc.vector.quantize_mx(out=xcv[:].bitcast(FP8X4), scales=xsv[:], in_=xpm[:])
+            xc[v] = xcv
+            xs[v] = xsv
+
+        def x_operand(v, u, neg):
+            o = ((4 if neg else 0) + u) * P
+            return xc[v][:, o : o + P].bitcast(FP8X4), xs[v][:, o : o + P]
+
+        acc = {}
+        r_sb = {}
+        a01 = {}
+
+        def store(ch, p, zt):
+            k0, n = CHUNKS[ch]
+            for q in range(4):
+                nc.sync.dma_start(out=out_view[p, q][:, :, k0 : k0 + n], in_=zt[:, q, :])
+
+        for idx in range(len(items)):
+            ch, v, u = items[idx]
+            k0, n = CHUNKS[ch]
+            if idx not in raws:
+                load_w(idx)
+            raw = raws[idx]
+            grp = wpool.tile([P, n, 4], BF16, tag="grp", bufs=GRP_BUFS, name="grp%d" % idx, align_bytes=64)
+            dst = grp[:].rearrange("p (c i) t -> p c t i", i=4)
+            src = raw[:].rearrange("p t (c i) -> p c t i", i=4)
+            if idx in V_REGROUP:
+                nc.vector.tensor_copy(out=dst, in_=src)
+            else:
+                nc.scalar.copy(out=dst, in_=src)
+            wc = wpool.tile([P, n], U32, tag="wc", bufs=CODE_BUFS, name="wc%d" % idx, align_bytes=64)
+            ws = wpool.tile([P, n], U8, tag="ws", bufs=CODE_BUFS, name="ws%d" % idx, align_bytes=64)
+            nc.vector.quantize_mx(
+                out=wc[:].bitcast(FP8X4), scales=ws[:], in_=grp[:].rearrange("p w j -> p (w j)")
+            )
+
+            eight = MODE8[ch] and v >= 2
+            if eight:
+                first = v == 2 and u == 0
+                last = v == 3 and u == 3
+                for p in range(4):
+                    for q0 in range(2):
+                        if first:
+                            acc[(p, q0)] = bank(2 * p + q0, "c%d_%d_%d" % (ch, p, q0))
+                        neg = sign_neg(p, u) != (v == 3 and q0 == 1)
+                        lhsT, lhsT_scale = x_operand(v, u, neg)
+                        nc.tensor.matmul_mx(
+                            out=acc[(p, q0)][:, 0:n], lhsT=lhsT, lhsT_scale=lhsT_scale,
+                            rhs=wc[:].bitcast(FP8X4), rhs_scale=ws[:], start=first, stop=last,
+                        )
+            else:
+                first = u == 0
+                last = u == 3
+                for p in range(4):
+                    if first:
+                        acc[p] = bank(4 * (v % 2) + p, "r%d_%d_%d" % (ch, v, p))
+                    lhsT, lhsT_scale = x_operand(v, u, sign_neg(p, u))
+                    nc.tensor.matmul_mx(
+                        out=acc[p][:, 0:n], lhsT=lhsT, lhsT_scale=lhsT_scale,
+                        rhs=wc[:].bitcast(FP8X4), rhs_scale=ws[:], start=first, stop=last,
+                    )
+            if not last:
+                continue
+
+            for p in range(4):
+                if eight:
+                    zt = hpool.tile([P, 4, n], F32, tag="zt", bufs=4, name="zt%d_%d" % (ch, p))
+                    for q0 in range(2):
+                        for q1 in range(2):
+                            nc.vector.scalar_tensor_tensor(
+                                out=zt[:, 2 * q1 + q0, :], in0=acc[(p, q0)][:, 0:n],
+                                scalar=(-SCALE if q1 else SCALE), in1=a01[(ch, p)][:, q0, :],
+                                op0=ALU.mult, op1=ALU.add,
+                            )
+                    store(ch, p, zt)
+                elif v == 0:
+                    r = hpool.tile([P, n], F32, tag="r", bufs=6, name="r0_%d_%d" % (ch, p))
+                    nc.vector.scalar_tensor_tensor(
+                        out=r[:], in0=acc[p][:, 0:n], scalar=SCALE, in1=bias_bc[:, k0 : k0 + n],
+                        op0=ALU.mult, op1=ALU.add,
+                    )
+                    r_sb[p] = r
+                elif v == 2:
+                    r = hpool.tile([P, n], F32, tag="r", bufs=6, name="r2_%d_%d" % (ch, p))
+                    nc.scalar.mul(out=r[:], in_=acc[p][:, 0:n], mul=SCALE)
+                    r_sb[p] = r
+                else:
+                    if v == 1:
+                        a = hpool.tile([P, 2, n], F32, tag="a01", bufs=6, name="a01_%d_%d" % (ch, p))
+                        a01[(ch, p)] = a
+                    else:
+                        a = hpool.tile([P, 2, n], F32, tag="a23", bufs=3, name="a23_%d_%d" % (ch, p))
+                    for q0 in range(2):
+                        nc.vector.scalar_tensor_tensor(
+                            out=a[:, q0, :], in0=acc[p][:, 0:n],
+                            scalar=(-SCALE if q0 else SCALE), in1=r_sb[p][:],
+                            op0=ALU.mult, op1=ALU.add,
+                        )
+                    if v == 3:
+                        zt = hpool.tile([P, 4, n], F32, tag="zt", bufs=4, name="zt%d_%d" % (ch, p))
+                        nc.vector.tensor_tensor(out=zt[:, 0:2, :], in0=a01[(ch, p)][:], in1=a[:], op=ALU.add)
+                        nc.vector.tensor_tensor(out=zt[:, 2:4, :], in0=a01[(ch, p)][:], in1=a[:], op=ALU.subtract)
+                        store(ch, p, zt)

@@ -1,8 +1,6 @@
 from contextlib import ExitStack
 
-import concourse.bass as bass
 import concourse.mybir as mybir
-import concourse.tile as tile
 from concourse.masks import make_identity
 
 F32 = mybir.dt.float32
@@ -16,14 +14,16 @@ P = 128
 T = 16
 C = 512
 K = 1024
+H = 512
 FLOPS = 2 * T * P * C * K
 
-CHUNKS = [(0, 512), (512, 512)]
-MODE8 = [True, True]
-V_REGROUP = (3, 7, 19, 23)
-RAW_BUFS = 6
-GRP_BUFS = 4
+PIN = True
+S_COLS = (512, 512, 800, 512, 800, 864, 864, 800, 512, 864, 864, 864, 864, 512, 512, 512)
+X_SLOT = {0: 0, 2: 1, 4: 2, 7: 3}
+RAW_BUFS = 4
+GRP_BUFS = 3
 CODE_BUFS = 10
+ZT_BUFS = 8
 SCALE = 1.0 / 16.0
 
 
@@ -35,175 +35,238 @@ def sign_neg(a, b):
 def tile_iwht3layer_pa_kernel(tc, trans, weight, bias, out):
     nc = tc.nc
     with ExitStack() as ctx:
+        if PIN:
+            ctx.enter_context(tc.manual_schedule())
         const = ctx.enter_context(tc.tile_pool(name="const", bufs=1))
         xpool = ctx.enter_context(tc.tile_pool(name="xpool", bufs=1))
         wpool = ctx.enter_context(tc.tile_pool(name="wpool", bufs=2))
         hpool = ctx.enter_context(tc.tile_pool(name="hpool", bufs=2))
         psum = ctx.enter_context(tc.psum_pool(name="psum", bufs=1))
 
-        ident = const.tile([P, P], F32, name="ident")
-        make_identity(nc, ident[:])
-        bias_bc = const.tile([P, K], BF16, name="bias_bc")
-        nc.gpsimd.dma_start(
-            out=bias_bc[:],
-            in_=bias.rearrange("a b c k -> (a b c k)").partition_broadcast(P),
-        )
-
         x_view = trans.rearrange("(u v) b i j c -> v (b i j) u c", v=4)
         w_view = weight.rearrange("t (p j) k -> t p j k", j=4)
         out_view = out.rearrange("b (i p) (j q) k -> p q (b i) j k", p=4, q=4)
 
         def bank(b, name):
-            return psum.tile([P, 512], F32, tag="bank%d" % b, name=name)
+            return psum.tile([P, H], F32, tag="bank%d" % b, name=name)
 
-        items = []
-        for ch in range(len(CHUNKS)):
-            for v in range(4):
-                for u in range(4):
-                    items.append((ch, v, u))
+        zb = const.tile([P, K], BF16, name="zb")
+        nc.vector.memset(zb[:], 0.0)
+        ones = const.tile([P, P], BF16, name="ones")
+        nc.vector.memset(ones[:], 1.0)
+        nc.scalar.dma_start(out=zb[0:1, :], in_=bias.rearrange("a b c k -> (a b c) k"))
+        ident = const.tile([P, P], F32, name="ident")
+        make_identity(nc, ident[:])
+        bias_bc = const.tile([P, K], BF16, name="bias_bc")
 
         raws = {}
 
-        def load_w(idx):
-            ch, v, u = items[idx]
-            k0, n = CHUNKS[ch]
-            raw = wpool.tile([P, 4, n], BF16, tag="raw", bufs=RAW_BUFS, name="raw%d" % idx)
-            nc.sync.dma_start(out=raw[:], in_=w_view[4 * u + v][:, :, k0 : k0 + n])
-            raws[idx] = raw
+        def load_w(s):
+            v, u = s // 4, s % 4
+            raw = wpool.tile([P, 4, K], BF16, tag="raw", bufs=RAW_BUFS, name="raw%d" % s)
+            nc.sync.dma_start(out=raw[:], in_=w_view[4 * u + v])
+            raws[s] = raw
 
         xraw = {}
 
         def load_x(v):
-            xr = xpool.tile([P, 4 * C], BF16, name="xraw%d" % v)
+            xr = hpool.tile([P, 4 * C], BF16, tag="zt", bufs=ZT_BUFS, name="xraw%d" % v)
             nc.sync.dma_start(out=xr[:].rearrange("p (u c) -> p u c", u=4), in_=x_view[v])
             xraw[v] = xr
 
-        for v in range(4):
-            load_x(v)
-            load_w(v)
+        load_w(0)
+        load_x(0)
+        load_x(1)
+        load_w(1)
+        load_x(2)
+        load_x(3)
+        load_w(2)
+        load_w(3)
 
+        xg = {}
         xc = {}
         xs = {}
-        for v in range(4):
+
+        def x_transpose(v):
             xw = xraw[v][:].bitcast(F32).rearrange("p (u w h) -> p u h w", u=4, h=2)
-            xpm = xpool.tile([P, 2 * 4 * P * 4], BF16, tag="xpm", bufs=2, name="xpm%d" % v, align_bytes=64)
-            xpm_w = xpm[:].bitcast(F32).rearrange("p (s u m h) -> p s u m h", s=2, u=4, h=2)
+            g_t = xpool.tile([P, 4 * P * 4], BF16, name="xg%d" % v, align_bytes=64)
+            g_w = g_t[:].bitcast(F32).rearrange("p (u m h) -> p u m h", u=4, h=2)
             for g in range(2):
                 xt = bank(2 * v + g, "xt%d_%d" % (v, g))
                 xt4 = xt[:].rearrange("p (u h m) -> p u h m", u=2, h=2)
                 for u2 in range(2):
                     for h in range(2):
                         nc.tensor.transpose(xt4[:, u2, h, :], xw[:, 2 * g + u2, h, :], ident[:])
-                src = xt[:].rearrange("p (u h m) -> p u m h", u=2, h=2)
-                dst = xpm_w[:, 0, 2 * g : 2 * g + 2, :, :]
-                if g == 0:
-                    nc.scalar.copy(out=dst, in_=src)
-                else:
-                    nc.vector.tensor_copy(out=dst, in_=src)
-            half = 4 * P * 4
-            nc.vector.tensor_scalar_mul(out=xpm[:, half : 2 * half], in0=xpm[:, 0:half], scalar1=-1.0)
+                nc.scalar.copy(
+                    out=g_w[:, 2 * g : 2 * g + 2, :, :],
+                    in_=xt[:].rearrange("p (u h m) -> p u m h", u=2, h=2),
+                )
+            xg[v] = g_t
+
+        def x_quantise(v):
             xcv = xpool.tile([P, 2 * 4 * P], U32, name="xc%d" % v, align_bytes=64)
             xsv = xpool.tile([P, 2 * 4 * P], U8, name="xs%d" % v, align_bytes=64)
-            nc.vector.quantize_mx(out=xcv[:].bitcast(FP8X4), scales=xsv[:], in_=xpm[:])
+            xn = xpool.tile([P, 4 * P * 4], BF16, tag="xn", bufs=2, name="xn%d" % v, align_bytes=64)
+            nc.vector.tensor_scalar_mul(out=xn[:], in0=xg[v][:], scalar1=-1.0)
+            nc.vector.quantize_mx(out=xcv[:, 0:H].bitcast(FP8X4), scales=xsv[:, 0:H], in_=xg[v][:])
+            nc.vector.quantize_mx(out=xcv[:, H : 2 * H].bitcast(FP8X4), scales=xsv[:, H : 2 * H], in_=xn[:])
             xc[v] = xcv
             xs[v] = xsv
 
-        def x_operand(v, u, neg):
-            o = ((4 if neg else 0) + u) * P
-            return xc[v][:, o : o + P].bitcast(FP8X4), xs[v][:, o : o + P]
+        grps = {}
+        wcs = {}
+        wss = {}
+
+        def regroup(s):
+            raw = raws[s]
+            grp = wpool.tile([P, K, 4], BF16, tag="grp", bufs=GRP_BUFS, name="grp%d" % s, align_bytes=64)
+            cut = S_COLS[s]
+            nc.scalar.copy(
+                out=grp[:, 0:cut, :].rearrange("p (c i) t -> p c t i", i=4),
+                in_=raw[:, :, 0:cut].rearrange("p t (c i) -> p c t i", i=4),
+            )
+            nc.vector.tensor_copy(
+                out=grp[:, cut:K, :].rearrange("p (c i) t -> p c t i", i=4),
+                in_=raw[:, :, cut:K].rearrange("p t (c i) -> p c t i", i=4),
+            )
+            grps[s] = grp
+
+        def quantise(s):
+            wc = wpool.tile([P, K], U32, tag="wc", bufs=CODE_BUFS, name="wc%d" % s, align_bytes=64)
+            ws = wpool.tile([P, K], U8, tag="ws", bufs=CODE_BUFS, name="ws%d" % s, align_bytes=64)
+            nc.vector.quantize_mx(
+                out=wc[:].bitcast(FP8X4), scales=ws[:], in_=grps[s][:].rearrange("p w j -> p (w j)")
+            )
+            wcs[s] = wc
+            wss[s] = ws
 
         acc = {}
-        r_sb = {}
-        a01 = {}
 
-        def store(ch, p, zt):
-            k0, n = CHUNKS[ch]
-            for q in range(4):
-                nc.sync.dma_start(out=out_view[p, q][:, :, k0 : k0 + n], in_=zt[:, q, :])
-
-        for idx in range(len(items)):
-            ch, v, u = items[idx]
-            k0, n = CHUNKS[ch]
-            if idx not in raws:
-                load_w(idx)
-            raw = raws[idx]
-            grp = wpool.tile([P, n, 4], BF16, tag="grp", bufs=GRP_BUFS, name="grp%d" % idx, align_bytes=64)
-            dst = grp[:].rearrange("p (c i) t -> p c t i", i=4)
-            src = raw[:].rearrange("p t (c i) -> p c t i", i=4)
-            if idx in V_REGROUP:
-                nc.vector.tensor_copy(out=dst, in_=src)
-            else:
-                nc.scalar.copy(out=dst, in_=src)
-            wc = wpool.tile([P, n], U32, tag="wc", bufs=CODE_BUFS, name="wc%d" % idx, align_bytes=64)
-            ws = wpool.tile([P, n], U8, tag="ws", bufs=CODE_BUFS, name="ws%d" % idx, align_bytes=64)
-            nc.vector.quantize_mx(
-                out=wc[:].bitcast(FP8X4), scales=ws[:], in_=grp[:].rearrange("p w j -> p (w j)")
+        def mx_pass(b, s, h, neg, start, stop):
+            v, u = s // 4, s % 4
+            o = ((4 if neg else 0) + u) * P
+            nc.tensor.matmul_mx(
+                out=acc[b][:],
+                lhsT=xc[v][:, o : o + P].bitcast(FP8X4),
+                lhsT_scale=xs[v][:, o : o + P],
+                rhs=wcs[s][:, h * H : (h + 1) * H].bitcast(FP8X4),
+                rhs_scale=wss[s][:, h * H : (h + 1) * H],
+                start=start,
+                stop=stop,
             )
 
-            eight = MODE8[ch] and v >= 2
-            if eight:
-                first = v == 2 and u == 0
-                last = v == 3 and u == 3
-                for p in range(4):
-                    for q0 in range(2):
-                        if first:
-                            acc[(p, q0)] = bank(2 * p + q0, "c%d_%d_%d" % (ch, p, q0))
-                        neg = sign_neg(p, u) != (v == 3 and q0 == 1)
-                        lhsT, lhsT_scale = x_operand(v, u, neg)
-                        nc.tensor.matmul_mx(
-                            out=acc[(p, q0)][:, 0:n], lhsT=lhsT, lhsT_scale=lhsT_scale,
-                            rhs=wc[:].bitcast(FP8X4), rhs_scale=ws[:], start=first, stop=last,
-                        )
-            else:
-                first = u == 0
-                last = u == 3
-                for p in range(4):
-                    if first:
-                        acc[p] = bank(4 * (v % 2) + p, "r%d_%d_%d" % (ch, v, p))
-                    lhsT, lhsT_scale = x_operand(v, u, sign_neg(p, u))
-                    nc.tensor.matmul_mx(
-                        out=acc[p][:, 0:n], lhsT=lhsT, lhsT_scale=lhsT_scale,
-                        rhs=wc[:].bitcast(FP8X4), rhs_scale=ws[:], start=first, stop=last,
-                    )
-            if not last:
-                continue
+        def passes_of(s):
+            v, u = s // 4, s % 4
+            res = []
+            for h in range(2):
+                if v < 2:
+                    for p in range(4):
+                        res.append((4 * h + p, h, sign_neg(p, u), u == 0, u == 3))
+                else:
+                    for p in range(2):
+                        for q0 in range(2):
+                            neg = sign_neg(p, u) != (v == 3 and q0 == 1)
+                            res.append((4 * h + 2 * p + q0, h, neg, s == 8, s == 15))
+            return res
 
-            for p in range(4):
-                if eight:
-                    zt = hpool.tile([P, 4, n], F32, tag="zt", bufs=4, name="zt%d_%d" % (ch, p))
-                    for q0 in range(2):
-                        for q1 in range(2):
-                            nc.vector.scalar_tensor_tensor(
-                                out=zt[:, 2 * q1 + q0, :], in0=acc[(p, q0)][:, 0:n],
-                                scalar=(-SCALE if q1 else SCALE), in1=a01[(ch, p)][:, q0, :],
-                                op0=ALU.mult, op1=ALU.add,
-                            )
-                    store(ch, p, zt)
-                elif v == 0:
-                    r = hpool.tile([P, n], F32, tag="r", bufs=6, name="r0_%d_%d" % (ch, p))
+        def bank_slot(s, b):
+            if s < 4:
+                return 0
+            if s < 8:
+                return 5 + b // 4
+            return 9 + b // 2
+
+        todo = []
+        r0 = {}
+        a01 = {}
+
+        def evac_r0(b):
+            h = b // 4
+            r = hpool.tile([P, H], F32, tag="r0", bufs=8, name="r0_%d" % b)
+            nc.vector.scalar_tensor_tensor(
+                out=r[:], in0=acc[b][:], scalar=SCALE, in1=bias_bc[:, h * H : (h + 1) * H],
+                op0=ALU.mult, op1=ALU.add,
+            )
+            r0[b] = r
+
+        def evac_a(b):
+            a = hpool.tile([P, 2, H], F32, tag="a01", bufs=8, name="a01_%d" % b)
+            for q0 in range(2):
+                nc.vector.scalar_tensor_tensor(
+                    out=a[:, q0, :], in0=acc[b][:], scalar=(-SCALE if q0 else SCALE), in1=r0[b][:],
+                    op0=ALU.mult, op1=ALU.add,
+                )
+            a01[b] = a
+
+        for slot in range(T + 1):
+            if slot < T:
+                regroup(slot)
+                if slot + RAW_BUFS < T:
+                    load_w(slot + RAW_BUFS)
+            if slot == 0:
+                x_transpose(0)
+                x_transpose(1)
+            if slot == 1:
+                x_transpose(2)
+                x_transpose(3)
+                for h in range(2):
+                    bb = bank(h, "biasb%d" % h)
+                    nc.tensor.matmul(out=bb[:], lhsT=ones[:], rhs=zb[:, h * H : (h + 1) * H], start=True, stop=True)
+                    nc.scalar.copy(out=bias_bc[:, h * H : (h + 1) * H], in_=bb[:])
+            if slot in X_SLOT:
+                x_quantise(X_SLOT[slot])
+            if slot in (5, 6):
+                for b in range(4 * (slot - 5), 4 * (slot - 5) + 4):
+                    evac_r0(b)
+            if 9 <= slot <= 12:
+                for b in range(2 * (slot - 9), 2 * (slot - 9) + 2):
+                    evac_a(b)
+            if slot >= 1:
+                quantise(slot - 1)
+                todo.extend([(slot - 1, e) for e in passes_of(slot - 1)])
+                later = []
+                for s, e in todo:
+                    b, h, neg, start, stop = e
+                    if bank_slot(s, b) > slot:
+                        later.append((s, e))
+                        continue
+                    if start:
+                        acc[b] = bank(b, "acc%d_%d" % (s, b))
+                    mx_pass(b, s, h, neg, start, stop)
+                todo = later
+
+        def z_pair(p, q0, banks_by_half):
+            zts = []
+            for q1 in range(2):
+                zt_t = hpool.tile([P, K], F32, tag="zt", bufs=ZT_BUFS, name="zt%d_%d" % (p, 2 * q1 + q0))
+                zts.append(zt_t)
+            for h in range(2):
+                b = banks_by_half[h]
+                for q1 in range(2):
                     nc.vector.scalar_tensor_tensor(
-                        out=r[:], in0=acc[p][:, 0:n], scalar=SCALE, in1=bias_bc[:, k0 : k0 + n],
+                        out=zts[q1][:, h * H : (h + 1) * H], in0=acc[b][:],
+                        scalar=(-SCALE if q1 else SCALE), in1=a01[4 * h + p][:, q0, :],
                         op0=ALU.mult, op1=ALU.add,
                     )
-                    r_sb[p] = r
-                elif v == 2:
-                    r = hpool.tile([P, n], F32, tag="r", bufs=6, name="r2_%d_%d" % (ch, p))
-                    nc.scalar.mul(out=r[:], in_=acc[p][:, 0:n], mul=SCALE)
-                    r_sb[p] = r
-                else:
-                    if v == 1:
-                        a = hpool.tile([P, 2, n], F32, tag="a01", bufs=6, name="a01_%d_%d" % (ch, p))
-                        a01[(ch, p)] = a
-                    else:
-                        a = hpool.tile([P, 2, n], F32, tag="a23", bufs=3, name="a23_%d_%d" % (ch, p))
-                    for q0 in range(2):
-                        nc.vector.scalar_tensor_tensor(
-                            out=a[:, q0, :], in0=acc[p][:, 0:n],
-                            scalar=(-SCALE if q0 else SCALE), in1=r_sb[p][:],
-                            op0=ALU.mult, op1=ALU.add,
-                        )
-                    if v == 3:
-                        zt = hpool.tile([P, 4, n], F32, tag="zt", bufs=4, name="zt%d_%d" % (ch, p))
-                        nc.vector.tensor_tensor(out=zt[:, 0:2, :], in0=a01[(ch, p)][:], in1=a[:], op=ALU.add)
-                        nc.vector.tensor_tensor(out=zt[:, 2:4, :], in0=a01[(ch, p)][:], in1=a[:], op=ALU.subtract)
-                        store(ch, p, zt)
+            for q1 in range(2):
+                nc.sync.dma_start(out=out_view[p, 2 * q1 + q0], in_=zts[q1][:])
+
+        freed = []
+        for p in range(2):
+            for q0 in range(2):
+                pair = [2 * p + q0, 4 + 2 * p + q0]
+                z_pair(p, q0, pair)
+                freed.append(pair)
+        late = []
+        for p in range(2, 4):
+            for q0 in range(2):
+                pair = freed[len(late)]
+                for h in range(2):
+                    b = pair[h]
+                    acc[b] = bank(b, "tail%d_%d_%d" % (p, q0, h))
+                    for s in range(8, 16):
+                        neg = sign_neg(p, s % 4) != (s >= 12 and q0 == 1)
+                        mx_pass(b, s, h, neg, s == 8, s == 15)
+                late.append((p, q0, pair))
+        for p, q0, pair in late:
+            z_pair(p, q0, pair)

@@ -74,7 +74,10 @@ def tile_iwht3layer_pa_kernel(tc, trans, weight, bias, out):
             nc.sync.dma_start(out=xr[:].rearrange("p (u c) -> p u c", u=4), in_=x_view[v])
             xraw[v] = xr
 
-        load_w(0)
+        raw0 = wpool.tile([P, 4, K], BF16, tag="raw", bufs=RAW_BUFS, name="raw0")
+        for h in range(2):
+            nc.sync.dma_start(out=raw0[:, :, h * H : (h + 1) * H], in_=w_view[0][:, :, h * H : (h + 1) * H])
+        raws[0] = raw0
         load_x(0)
         load_x(1)
         load_w(1)
@@ -89,7 +92,7 @@ def tile_iwht3layer_pa_kernel(tc, trans, weight, bias, out):
 
         def x_transpose(v):
             xw = xraw[v][:].bitcast(F32).rearrange("p (u w h) -> p u h w", u=4, h=2)
-            g_t = xpool.tile([P, 4 * P * 4], BF16, name="xg%d" % v, align_bytes=64)
+            g_t = xpool.tile([P, 4 * P * 4], BF16, tag="xg", bufs=4, name="xg%d" % v, align_bytes=64)
             g_w = g_t[:].bitcast(F32).rearrange("p (u m h) -> p u m h", u=4, h=2)
             for g in range(2):
                 xt = bank(2 * v + g, "xt%d_%d" % (v, g))
@@ -190,13 +193,14 @@ def tile_iwht3layer_pa_kernel(tc, trans, weight, bias, out):
             r0[b] = r
 
         def evac_a(b):
-            a = hpool.tile([P, 2, H], F32, tag="a01", bufs=8, name="a01_%d" % b)
+            h, p = b // 4, b % 4
+            if h == 0:
+                a01[p] = hpool.tile([P, 2, 2, H], F32, tag="a01", bufs=4, name="a01_%d" % p)
             for q0 in range(2):
                 nc.vector.scalar_tensor_tensor(
-                    out=a[:, q0, :], in0=acc[b][:], scalar=(-SCALE if q0 else SCALE), in1=r0[b][:],
+                    out=a01[p][:, q0, h, :], in0=acc[b][:], scalar=(-SCALE if q0 else SCALE), in1=r0[b][:],
                     op0=ALU.mult, op1=ALU.add,
                 )
-            a01[b] = a
 
         for slot in range(T + 1):
             if slot < T:
@@ -245,28 +249,48 @@ def tile_iwht3layer_pa_kernel(tc, trans, weight, bias, out):
                 for q1 in range(2):
                     nc.vector.scalar_tensor_tensor(
                         out=zts[q1][:, h * H : (h + 1) * H], in0=acc[b][:],
-                        scalar=(-SCALE if q1 else SCALE), in1=a01[4 * h + p][:, q0, :],
+                        scalar=(-SCALE if q1 else SCALE), in1=a01[p][:, q0, h, :],
                         op0=ALU.mult, op1=ALU.add,
                     )
             for q1 in range(2):
                 nc.sync.dma_start(out=out_view[p, 2 * q1 + q0], in_=zts[q1][:])
 
-        freed = []
-        for p in range(2):
+        def group(b, name, p, q0, h, tiles):
+            acc[b] = bank(b, name)
+            for s in tiles:
+                neg = sign_neg(p, s % 4) != (s >= 12 and q0 == 1)
+                mx_pass(b, s, h, neg, s == tiles[0], s == tiles[-1])
+
+        z_pair(0, 0, [0, 4])
+        r2s = []
+        for h in range(2):
+            group(4 * h, "r2_%d" % h, 2, 0, h, list(range(8, 12)))
+            r = hpool.tile([P, H], F32, tag="r0", bufs=8, name="r2s_%d" % h)
+            nc.scalar.mul(out=r[:], in_=acc[4 * h][:], mul=SCALE)
+            r2s.append(r)
+        z_pair(0, 1, [1, 5])
+        a23 = wpool.tile([P, 2, 2, H], F32, tag="grp", bufs=GRP_BUFS, name="a23", align_bytes=64)
+        for h in range(2):
+            group(4 * h + 1, "r3_%d" % h, 2, 0, h, list(range(12, 16)))
             for q0 in range(2):
-                pair = [2 * p + q0, 4 + 2 * p + q0]
-                z_pair(p, q0, pair)
-                freed.append(pair)
-        late = []
-        for p in range(2, 4):
-            for q0 in range(2):
-                pair = freed[len(late)]
-                for h in range(2):
-                    b = pair[h]
-                    acc[b] = bank(b, "tail%d_%d_%d" % (p, q0, h))
-                    for s in range(8, 16):
-                        neg = sign_neg(p, s % 4) != (s >= 12 and q0 == 1)
-                        mx_pass(b, s, h, neg, s == 8, s == 15)
-                late.append((p, q0, pair))
-        for p, q0, pair in late:
-            z_pair(p, q0, pair)
+                nc.vector.scalar_tensor_tensor(
+                    out=a23[:, q0, h, :], in0=acc[4 * h + 1][:], scalar=(-SCALE if q0 else SCALE), in1=r2s[h][:],
+                    op0=ALU.mult, op1=ALU.add,
+                )
+        for q0 in range(2):
+            for q1 in range(2):
+                zt_t = xpool.tile([P, K], F32, tag="xg", bufs=4, name="zt2_%d" % (2 * q1 + q0), align_bytes=64)
+                nc.gpsimd.tensor_tensor(
+                    out=zt_t[:],
+                    in0=a01[2][:, q0, :, :].rearrange("p h k -> p (h k)"),
+                    in1=a23[:, q0, :, :].rearrange("p h k -> p (h k)"),
+                    op=(ALU.subtract if q1 else ALU.add),
+                )
+                nc.scalar.dma_start(out=out_view[2, 2 * q1 + q0], in_=zt_t[:])
+        for q0 in range(2):
+            for h in range(2):
+                group(4 * h + q0, "c3_%d_%d" % (q0, h), 3, q0, h, list(range(8, 16)))
+        z_pair(1, 0, [2, 6])
+        z_pair(1, 1, [3, 7])
+        z_pair(3, 0, [0, 4])
+        z_pair(3, 1, [1, 5])

@@ -18,12 +18,17 @@ H = 512
 FLOPS = 2 * T * P * C * K
 
 PIN = True
-S_COLS = (512, 512, 800, 512, 800, 864, 864, 800, 512, 864, 864, 864, 864, 512, 512, 512)
+CHUNKS = ((0, 512), (512, 256), (768, 256))
+S_COLS = (448, 448, 736, 448, 736, 800, 800, 736)
+ITEM_V = {}
 X_SLOT = {0: 0, 2: 1, 4: 2, 7: 3}
-RAW_BUFS = 4
+RAW_BUFS = 8
 GRP_BUFS = 3
-CODE_BUFS = 10
-ZT_BUFS = 8
+CODE_BUFS = 3
+ITEM_CODE_BUFS = 10
+LAGS1 = (0, 0, 0, 0, 1, 1, 1, 1)
+LAGS = (0, 1, 2, 3, 4, 5, 6, 7)
+ZT_BUFS = 6
 SCALE = 1.0 / 16.0
 
 
@@ -50,6 +55,14 @@ def tile_iwht3layer_pa_kernel(tc, trans, weight, bias, out):
         def bank(b, name):
             return psum.tile([P, H], F32, tag="bank%d" % b, name=name)
 
+        units = []
+        for s in range(8):
+            units.append((s, 0, K, S_COLS[s]))
+        for k0, w in CHUNKS:
+            for s in range(8, 16):
+                units.append((s, k0, w, w - ITEM_V.get(len(units), 0)))
+        n_units = len(units)
+
         zb = const.tile([P, K], BF16, name="zb")
         nc.vector.memset(zb[:], 0.0)
         ones = const.tile([P, P], BF16, name="ones")
@@ -61,30 +74,31 @@ def tile_iwht3layer_pa_kernel(tc, trans, weight, bias, out):
 
         raws = {}
 
-        def load_w(s):
+        def load_w(s, pieces):
             v, u = s // 4, s % 4
             raw = wpool.tile([P, 4, K], BF16, tag="raw", bufs=RAW_BUFS, name="raw%d" % s)
-            nc.sync.dma_start(out=raw[:], in_=w_view[4 * u + v])
+            step = K // pieces
+            for i in range(pieces):
+                nc.sync.dma_start(
+                    out=raw[:, :, i * step : (i + 1) * step], in_=w_view[4 * u + v][:, :, i * step : (i + 1) * step]
+                )
             raws[s] = raw
 
         xraw = {}
 
         def load_x(v):
-            xr = hpool.tile([P, 4 * C], BF16, tag="zt", bufs=ZT_BUFS, name="xraw%d" % v)
+            xr = hpool.tile([P, 4 * C], BF16, tag="a01", bufs=4, name="xraw%d" % v)
             nc.sync.dma_start(out=xr[:].rearrange("p (u c) -> p u c", u=4), in_=x_view[v])
             xraw[v] = xr
 
-        raw0 = wpool.tile([P, 4, K], BF16, tag="raw", bufs=RAW_BUFS, name="raw0")
-        for h in range(2):
-            nc.sync.dma_start(out=raw0[:, :, h * H : (h + 1) * H], in_=w_view[0][:, :, h * H : (h + 1) * H])
-        raws[0] = raw0
+        load_w(0, 2)
         load_x(0)
         load_x(1)
-        load_w(1)
+        load_w(1, 1)
         load_x(2)
         load_x(3)
-        load_w(2)
-        load_w(3)
+        for s in range(2, 8):
+            load_w(s, 1)
 
         xg = {}
         xc = {}
@@ -92,7 +106,7 @@ def tile_iwht3layer_pa_kernel(tc, trans, weight, bias, out):
 
         def x_transpose(v):
             xw = xraw[v][:].bitcast(F32).rearrange("p (u w h) -> p u h w", u=4, h=2)
-            g_t = xpool.tile([P, 4 * P * 4], BF16, tag="xg", bufs=4, name="xg%d" % v, align_bytes=64)
+            g_t = xpool.tile([P, 4 * P * 4], BF16, tag="xg", bufs=ZT_BUFS, name="xg%d" % v, align_bytes=64)
             g_w = g_t[:].bitcast(F32).rearrange("p (u m h) -> p u m h", u=4, h=2)
             for g in range(2):
                 xt = bank(2 * v + g, "xt%d_%d" % (v, g))
@@ -109,7 +123,7 @@ def tile_iwht3layer_pa_kernel(tc, trans, weight, bias, out):
         def x_quantise(v):
             xcv = xpool.tile([P, 2 * 4 * P], U32, name="xc%d" % v, align_bytes=64)
             xsv = xpool.tile([P, 2 * 4 * P], U8, name="xs%d" % v, align_bytes=64)
-            xn = xpool.tile([P, 4 * P * 4], BF16, tag="xn", bufs=2, name="xn%d" % v, align_bytes=64)
+            xn = xpool.tile([P, 4 * P * 4], BF16, tag="xn", bufs=1, name="xn%d" % v, align_bytes=64)
             nc.vector.tensor_scalar_mul(out=xn[:], in0=xg[v][:], scalar1=-1.0)
             nc.vector.quantize_mx(out=xcv[:, 0:H].bitcast(FP8X4), scales=xsv[:, 0:H], in_=xg[v][:])
             nc.vector.quantize_mx(out=xcv[:, H : 2 * H].bitcast(FP8X4), scales=xsv[:, H : 2 * H], in_=xn[:])
@@ -120,64 +134,71 @@ def tile_iwht3layer_pa_kernel(tc, trans, weight, bias, out):
         wcs = {}
         wss = {}
 
-        def regroup(s):
+        def regroup(n):
+            s, k0, w, cut = units[n]
             raw = raws[s]
-            grp = wpool.tile([P, K, 4], BF16, tag="grp", bufs=GRP_BUFS, name="grp%d" % s, align_bytes=64)
-            cut = S_COLS[s]
+            grp = wpool.tile([P, w, 4], BF16, tag="grp", bufs=GRP_BUFS, name="grp%d" % n, align_bytes=64)
             nc.scalar.copy(
                 out=grp[:, 0:cut, :].rearrange("p (c i) t -> p c t i", i=4),
-                in_=raw[:, :, 0:cut].rearrange("p t (c i) -> p c t i", i=4),
+                in_=raw[:, :, k0 : k0 + cut].rearrange("p t (c i) -> p c t i", i=4),
             )
-            nc.vector.tensor_copy(
-                out=grp[:, cut:K, :].rearrange("p (c i) t -> p c t i", i=4),
-                in_=raw[:, :, cut:K].rearrange("p t (c i) -> p c t i", i=4),
-            )
-            grps[s] = grp
+            if cut < w:
+                nc.vector.tensor_copy(
+                    out=grp[:, cut:w, :].rearrange("p (c i) t -> p c t i", i=4),
+                    in_=raw[:, :, k0 + cut : k0 + w].rearrange("p t (c i) -> p c t i", i=4),
+                )
+            grps[n] = grp
 
-        def quantise(s):
-            wc = wpool.tile([P, K], U32, tag="wc", bufs=CODE_BUFS, name="wc%d" % s, align_bytes=64)
-            ws = wpool.tile([P, K], U8, tag="ws", bufs=CODE_BUFS, name="ws%d" % s, align_bytes=64)
+        def quantise(n):
+            s, k0, w, cut = units[n]
+            if n < 8:
+                wc = wpool.tile([P, w], U32, tag="wc", bufs=CODE_BUFS, name="wc%d" % n, align_bytes=64)
+                ws = wpool.tile([P, w], U8, tag="ws", bufs=CODE_BUFS, name="ws%d" % n, align_bytes=64)
+            else:
+                wc = wpool.tile([P, w], U32, tag="wci", bufs=ITEM_CODE_BUFS, name="wc%d" % n, align_bytes=64)
+                ws = wpool.tile([P, w], U8, tag="wsi", bufs=ITEM_CODE_BUFS, name="ws%d" % n, align_bytes=64)
             nc.vector.quantize_mx(
-                out=wc[:].bitcast(FP8X4), scales=ws[:], in_=grps[s][:].rearrange("p w j -> p (w j)")
+                out=wc[:].bitcast(FP8X4), scales=ws[:], in_=grps[n][:].rearrange("p w j -> p (w j)")
             )
-            wcs[s] = wc
-            wss[s] = ws
+            wcs[n] = wc
+            wss[n] = ws
 
         acc = {}
 
-        def mx_pass(b, s, h, neg, start, stop):
+        def mx_pass(b, n, c0, width, neg, start, stop):
+            s = units[n][0]
             v, u = s // 4, s % 4
             o = ((4 if neg else 0) + u) * P
             nc.tensor.matmul_mx(
-                out=acc[b][:],
+                out=acc[b][:, 0:width],
                 lhsT=xc[v][:, o : o + P].bitcast(FP8X4),
                 lhsT_scale=xs[v][:, o : o + P],
-                rhs=wcs[s][:, h * H : (h + 1) * H].bitcast(FP8X4),
-                rhs_scale=wss[s][:, h * H : (h + 1) * H],
+                rhs=wcs[n][:, c0 : c0 + width].bitcast(FP8X4),
+                rhs_scale=wss[n][:, c0 : c0 + width],
                 start=start,
                 stop=stop,
             )
 
-        def passes_of(s):
+        def passes_of(n):
+            s, k0, w, cut = units[n]
             v, u = s // 4, s % 4
             res = []
-            for h in range(2):
-                if v < 2:
+            if v < 2:
+                for h in range(2):
                     for p in range(4):
-                        res.append((4 * h + p, h, sign_neg(p, u), u == 0, u == 3))
-                else:
-                    for p in range(2):
-                        for q0 in range(2):
-                            neg = sign_neg(p, u) != (v == 3 and q0 == 1)
-                            res.append((4 * h + 2 * p + q0, h, neg, s == 8, s == 15))
+                        res.append((4 * h + p, h * H, H, sign_neg(p, u), u == 0, u == 3))
+            else:
+                for p in range(4):
+                    for q0 in range(2):
+                        neg = sign_neg(p, u) != (v == 3 and q0 == 1)
+                        res.append((2 * p + q0, 0, w, neg, s == 8, s == 15))
             return res
 
-        def bank_slot(s, b):
-            if s < 4:
-                return 0
-            if s < 8:
-                return 5 + b // 4
-            return 9 + b // 2
+        def pass_slot(n, b):
+            return n + 1 + (LAGS1[b] if n < 8 else LAGS[b])
+
+        def first_slot(n, b):
+            return max(pass_slot(n, b), pass_slot(n - 1, b) + 1)
 
         todo = []
         r0 = {}
@@ -195,18 +216,38 @@ def tile_iwht3layer_pa_kernel(tc, trans, weight, bias, out):
         def evac_a(b):
             h, p = b // 4, b % 4
             if h == 0:
-                a01[p] = hpool.tile([P, 2, 2, H], F32, tag="a01", bufs=4, name="a01_%d" % p)
+                a01[p] = hpool.tile([P, 2, K], F32, tag="a01", bufs=4, name="a01_%d" % p)
             for q0 in range(2):
                 nc.vector.scalar_tensor_tensor(
-                    out=a01[p][:, q0, h, :], in0=acc[b][:], scalar=(-SCALE if q0 else SCALE), in1=r0[b][:],
-                    op0=ALU.mult, op1=ALU.add,
+                    out=a01[p][:, q0, h * H : (h + 1) * H], in0=acc[b][:], scalar=(-SCALE if q0 else SCALE),
+                    in1=r0[b][:], op0=ALU.mult, op1=ALU.add,
                 )
 
-        for slot in range(T + 1):
-            if slot < T:
+        def evac_z(c, b):
+            k0, w = CHUNKS[c]
+            p, q0 = b // 2, b % 2
+            zt = xpool.tile([P, 2, w], F32, tag="xg", bufs=ZT_BUFS, name="zt%d_%d" % (c, b), align_bytes=64)
+            for q1 in range(2):
+                nc.vector.scalar_tensor_tensor(
+                    out=zt[:, q1, :], in0=acc[b][:, 0:w], scalar=(-SCALE if q1 else SCALE),
+                    in1=a01[p][:, q0, k0 : k0 + w], op0=ALU.mult, op1=ALU.add,
+                )
+            for q1 in range(2):
+                nc.sync.dma_start(out=out_view[p, 2 * q1 + q0][:, :, k0 : k0 + w], in_=zt[:, q1, :])
+
+        evac_at = {}
+        for b in range(8):
+            jobs = [(first_slot(4, b), 0, 0), (first_slot(8, b), 1, 0)]
+            for c in range(len(CHUNKS)):
+                jobs.append((first_slot(16 + 8 * c, b), 2, c))
+            for when, kind, c in jobs:
+                evac_at[when] = evac_at.get(when, []) + [(kind, c, b)]
+
+        for slot in range(n_units + max(LAGS) + 2):
+            if slot < n_units:
                 regroup(slot)
-                if slot + RAW_BUFS < T:
-                    load_w(slot + RAW_BUFS)
+                if slot < 8:
+                    load_w(slot + 8, 1)
             if slot == 0:
                 x_transpose(0)
                 x_transpose(1)
@@ -219,78 +260,30 @@ def tile_iwht3layer_pa_kernel(tc, trans, weight, bias, out):
                     nc.scalar.copy(out=bias_bc[:, h * H : (h + 1) * H], in_=bb[:])
             if slot in X_SLOT:
                 x_quantise(X_SLOT[slot])
-            if slot in (5, 6):
-                for b in range(4 * (slot - 5), 4 * (slot - 5) + 4):
-                    evac_r0(b)
-            if 9 <= slot <= 12:
-                for b in range(2 * (slot - 9), 2 * (slot - 9) + 2):
-                    evac_a(b)
-            if slot >= 1:
+            if 1 <= slot <= n_units:
                 quantise(slot - 1)
                 todo.extend([(slot - 1, e) for e in passes_of(slot - 1)])
-                later = []
-                for s, e in todo:
-                    b, h, neg, start, stop = e
-                    if bank_slot(s, b) > slot:
-                        later.append((s, e))
-                        continue
-                    if start:
-                        acc[b] = bank(b, "acc%d_%d" % (s, b))
-                    mx_pass(b, s, h, neg, start, stop)
-                todo = later
-
-        def z_pair(p, q0, banks_by_half):
-            zts = []
-            for q1 in range(2):
-                zt_t = hpool.tile([P, K], F32, tag="zt", bufs=ZT_BUFS, name="zt%d_%d" % (p, 2 * q1 + q0))
-                zts.append(zt_t)
-            for h in range(2):
-                b = banks_by_half[h]
-                for q1 in range(2):
-                    nc.vector.scalar_tensor_tensor(
-                        out=zts[q1][:, h * H : (h + 1) * H], in0=acc[b][:],
-                        scalar=(-SCALE if q1 else SCALE), in1=a01[p][:, q0, h, :],
-                        op0=ALU.mult, op1=ALU.add,
-                    )
-            for q1 in range(2):
-                nc.sync.dma_start(out=out_view[p, 2 * q1 + q0], in_=zts[q1][:])
-
-        def group(b, name, p, q0, h, tiles):
-            acc[b] = bank(b, name)
-            for s in tiles:
-                neg = sign_neg(p, s % 4) != (s >= 12 and q0 == 1)
-                mx_pass(b, s, h, neg, s == tiles[0], s == tiles[-1])
-
-        z_pair(0, 0, [0, 4])
-        r2s = []
-        for h in range(2):
-            group(4 * h, "r2_%d" % h, 2, 0, h, list(range(8, 12)))
-            r = hpool.tile([P, H], F32, tag="r0", bufs=8, name="r2s_%d" % h)
-            nc.scalar.mul(out=r[:], in_=acc[4 * h][:], mul=SCALE)
-            r2s.append(r)
-        z_pair(0, 1, [1, 5])
-        a23 = wpool.tile([P, 2, 2, H], F32, tag="grp", bufs=GRP_BUFS, name="a23", align_bytes=64)
-        for h in range(2):
-            group(4 * h + 1, "r3_%d" % h, 2, 0, h, list(range(12, 16)))
-            for q0 in range(2):
-                nc.vector.scalar_tensor_tensor(
-                    out=a23[:, q0, h, :], in0=acc[4 * h + 1][:], scalar=(-SCALE if q0 else SCALE), in1=r2s[h][:],
-                    op0=ALU.mult, op1=ALU.add,
-                )
-        for q0 in range(2):
-            for q1 in range(2):
-                zt_t = xpool.tile([P, K], F32, tag="xg", bufs=4, name="zt2_%d" % (2 * q1 + q0), align_bytes=64)
-                nc.gpsimd.tensor_tensor(
-                    out=zt_t[:],
-                    in0=a01[2][:, q0, :, :].rearrange("p h k -> p (h k)"),
-                    in1=a23[:, q0, :, :].rearrange("p h k -> p (h k)"),
-                    op=(ALU.subtract if q1 else ALU.add),
-                )
-                nc.scalar.dma_start(out=out_view[2, 2 * q1 + q0], in_=zt_t[:])
-        for q0 in range(2):
-            for h in range(2):
-                group(4 * h + q0, "c3_%d_%d" % (q0, h), 3, q0, h, list(range(8, 16)))
-        z_pair(1, 0, [2, 6])
-        z_pair(1, 1, [3, 7])
-        z_pair(3, 0, [0, 4])
-        z_pair(3, 1, [1, 5])
+            for kind, c, b in evac_at.get(slot, []):
+                if kind == 0:
+                    evac_r0(b)
+                elif kind == 1:
+                    evac_a(b)
+                else:
+                    evac_z(c, b)
+            now = []
+            later = []
+            held = set()
+            for n, e in todo:
+                b, start = e[0], e[4]
+                when = first_slot(n, b) if start else pass_slot(n, b)
+                if when > slot or b in held:
+                    later.append((n, e))
+                    held.add(b)
+                else:
+                    now.append((n, e))
+            for n, e in sorted(now, key=lambda t: (t[1][4], t[0], t[1][0])):
+                b, c0, width, neg, start, stop = e
+                if start:
+                    acc[b] = bank(b, "acc%d_%d" % (n, b))
+                mx_pass(b, n, c0, width, neg, start, stop)
+            todo = later

@@ -18,7 +18,7 @@ H = 512
 FLOPS = 2 * T * P * C * K
 
 PIN = True
-CHUNKS = ((0, 512), (512, 256), (768, 256))
+CHUNKS = ((0, 512), (512, 512))
 S_COLS = (448, 448, 736, 448, 736, 800, 800, 736)
 ITEM_V = {}
 X_SLOT = {0: 0, 2: 1, 4: 2, 7: 3}

@@ -18,8 +18,8 @@ H = 512
 FLOPS = 2 * T * P * C * K
 
 PIN = True
-CHUNKS = ((0, 512), (512, 512))
-S_COLS = (448, 448, 736, 448, 736, 800, 800, 736)
+CHUNKS = ((0, 512), (512, 256), (768, 256))
+S_COLS = (384, 384, 672, 384, 672, 736, 736, 672)
 ITEM_V = {}
 X_SLOT = {0: 0, 2: 1, 4: 2, 7: 3}
 RAW_BUFS = 8

@@ -17,9 +17,9 @@ K = 1024
 H = 512
 FLOPS = 2 * T * P * C * K
 
-PIN = True
+PIN = False
 CHUNKS = ((0, 512), (512, 256), (768, 256))
-S_COLS = (384, 384, 672, 384, 672, 736, 736, 672)
+S_COLS = (448, 448, 736, 448, 736, 800, 800, 736)
 ITEM_V = {}
 X_SLOT = {0: 0, 2: 1, 4: 2, 7: 3}
 RAW_BUFS = 8

@@ -139,13 +139,13 @@ def tile_iwht3layer_pa_kernel(tc, trans, weight, bias, out):
             raw = raws[s]
             grp = wpool.tile([P, w, 4], BF16, tag="grp", bufs=GRP_BUFS, name="grp%d" % n, align_bytes=64)
             nc.scalar.copy(
-                out=grp[:, 0:cut, :].rearrange("p (c i) t -> p c t i", i=4),
-                in_=raw[:, :, k0 : k0 + cut].rearrange("p t (c i) -> p c t i", i=4),
+                out=grp[:, 0:cut, :].rearrange("p (c i) t -> p c t i", i=8),
+                in_=raw[:, :, k0 : k0 + cut].rearrange("p t (c i) -> p c t i", i=8),
             )
             if cut < w:
                 nc.vector.tensor_copy(
-                    out=grp[:, cut:w, :].rearrange("p (c i) t -> p c t i", i=4),
-                    in_=raw[:, :, k0 + cut : k0 + w].rearrange("p t (c i) -> p c t i", i=4),
+                    out=grp[:, cut:w, :].rearrange("p (c i) t -> p c t i", i=8),
+                    in_=raw[:, :, k0 + cut : k0 + w].rearrange("p t (c i) -> p c t i", i=8),
                 )
             grps[n] = grp
 

@@ -20,7 +20,7 @@ FLOPS = 2 * T * P * C * K
 PIN = False
 CHUNKS = ((0, 512), (512, 256), (768, 256))
 S_COLS = (448, 448, 736, 448, 736, 800, 800, 736)
-ITEM_V = {}
+ITEM_V = dict([(n, 128) for n in range(8, 16)])
 X_SLOT = {0: 0, 2: 1, 4: 2, 7: 3}
 RAW_BUFS = 8
 GRP_BUFS = 3
@@ -63,6 +63,10 @@ def tile_iwht3layer_pa_kernel(tc, trans, weight, bias, out):
                 units.append((s, k0, w, w - ITEM_V.get(len(units), 0)))
         n_units = len(units)
 
+        warm_in = const.tile([P, 1], F32, name="warm_in")
+        nc.gpsimd.memset(warm_in[:], 0.0)
+        warm_out = const.tile([P, 1], F32, name="warm_out")
+        nc.scalar.copy(out=warm_out[:], in_=warm_in[:])
         zb = const.tile([P, K], BF16, name="zb")
         nc.vector.memset(zb[:], 0.0)
         ones = const.tile([P, P], BF16, name="ones")

@@ -67,11 +67,6 @@ def tile_iwht3layer_pa_kernel(tc, trans, weight, bias, out):
         nc.gpsimd.memset(warm_in[:], 0.0)
         warm_out = const.tile([P, 1], F32, name="warm_out")
         nc.scalar.copy(out=warm_out[:], in_=warm_in[:])
-        zb = const.tile([P, K], BF16, name="zb")
-        nc.vector.memset(zb[:], 0.0)
-        ones = const.tile([P, P], BF16, name="ones")
-        nc.vector.memset(ones[:], 1.0)
-        nc.scalar.dma_start(out=zb[0:1, :], in_=bias.rearrange("a b c k -> (a b c) k"))
         ident = const.tile([P, P], F32, name="ident")
         make_identity(nc, ident[:])
         bias_bc = const.tile([P, K], BF16, name="bias_bc")
@@ -101,7 +96,10 @@ def tile_iwht3layer_pa_kernel(tc, trans, weight, bias, out):
         load_w(1, 1)
         load_x(2)
         load_x(3)
-        for s in range(2, 8):
+        load_w(2, 1)
+        load_w(3, 1)
+        nc.sync.dma_start(out=bias_bc[:], in_=bias.rearrange("a b c k -> (a b c k)").partition_broadcast(P))
+        for s in range(4, 8):
             load_w(s, 1)
 
         xg = {}
@@ -237,7 +235,8 @@ def tile_iwht3layer_pa_kernel(tc, trans, weight, bias, out):
                     in1=a01[p][:, q0, k0 : k0 + w], op0=ALU.mult, op1=ALU.add,
                 )
             for q1 in range(2):
-                nc.sync.dma_start(out=out_view[p, 2 * q1 + q0][:, :, k0 : k0 + w], in_=zt[:, q1, :])
+                queue = nc.scalar if (c == len(CHUNKS) - 1 and q1 == 1) else nc.sync
+                queue.dma_start(out=out_view[p, 2 * q1 + q0][:, :, k0 : k0 + w], in_=zt[:, q1, :])
 
         evac_at = {}
         for b in range(8):
@@ -258,10 +257,6 @@ def tile_iwht3layer_pa_kernel(tc, trans, weight, bias, out):
             if slot == 1:
                 x_transpose(2)
                 x_transpose(3)
-                for h in range(2):
-                    bb = bank(h, "biasb%d" % h)
-                    nc.tensor.matmul(out=bb[:], lhsT=ones[:], rhs=zb[:, h * H : (h + 1) * H], start=True, stop=True)
-                    nc.scalar.copy(out=bias_bc[:, h * H : (h + 1) * H], in_=bb[:])
             if slot in X_SLOT:
                 x_quantise(X_SLOT[slot])
             if 1 <= slot <= n_units:

@@ -20,8 +20,8 @@ FLOPS = 2 * T * P * C * K
 PIN = False
 CHUNKS = ((0, 512), (512, 256), (768, 256))
 S_COLS = (448, 448, 736, 448, 736, 800, 800, 736)
-ITEM_V = dict([(n, 128) for n in range(8, 16)])
-X_SLOT = {0: 0, 2: 1, 4: 2, 7: 3}
+ITEM_V = dict([(n, 64) for n in range(8, 16)])
+X_SLOT = {0: 0, 2: 1, 8: 2, 10: 3}
 RAW_BUFS = 8
 GRP_BUFS = 3
 CODE_BUFS = 3

from contextlib import ExitStack

import concourse.mybir as mybir
from concourse.masks import make_identity

F32 = mybir.dt.float32
BF16 = mybir.dt.bfloat16
U32 = mybir.dt.uint32
U8 = mybir.dt.uint8
FP8X4 = mybir.dt.float8_e4m3fn_x4
ALU = mybir.AluOpType

P = 128
T = 16
C = 512
K = 1024
H = 512
FLOPS = 2 * T * P * C * K

PIN = False
CHUNKS = ((0, 512), (512, 256), (768, 256))
S_COLS = (448, 448, 736, 448, 736, 800, 800, 736)
ITEM_V = dict([(n, 64) for n in range(8, 16)])
X_SLOT = {0: 0, 2: 1, 8: 2, 10: 3}
RAW_BUFS = 8
GRP_BUFS = 3
CODE_BUFS = 3
ITEM_CODE_BUFS = 10
LAGS1 = (0, 0, 0, 0, 1, 1, 1, 1)
LAGS = (0, 1, 2, 3, 4, 5, 6, 7)
ZT_BUFS = 6
SCALE = 1.0 / 16.0


def sign_neg(a, b):
    x = a & b
    return ((x & 1) + ((x >> 1) & 1)) % 2 == 1


def tile_iwht3layer_pa_kernel(tc, trans, weight, bias, out):
    nc = tc.nc
    with ExitStack() as ctx:
        if PIN:
            ctx.enter_context(tc.manual_schedule())
        const = ctx.enter_context(tc.tile_pool(name="const", bufs=1))
        xpool = ctx.enter_context(tc.tile_pool(name="xpool", bufs=1))
        wpool = ctx.enter_context(tc.tile_pool(name="wpool", bufs=2))
        hpool = ctx.enter_context(tc.tile_pool(name="hpool", bufs=2))
        psum = ctx.enter_context(tc.psum_pool(name="psum", bufs=1))

        x_view = trans.rearrange("(u v) b i j c -> v (b i j) u c", v=4)
        w_view = weight.rearrange("t (p j) k -> t p j k", j=4)
        out_view = out.rearrange("b (i p) (j q) k -> p q (b i) j k", p=4, q=4)

        def bank(b, name):
            return psum.tile([P, H], F32, tag="bank%d" % b, name=name)

        units = []
        for s in range(8):
            units.append((s, 0, K, S_COLS[s]))
        for k0, w in CHUNKS:
            for s in range(8, 16):
                units.append((s, k0, w, w - ITEM_V.get(len(units), 0)))
        n_units = len(units)

        warm_in = const.tile([P, 1], F32, name="warm_in")
        nc.gpsimd.memset(warm_in[:], 0.0)
        warm_out = const.tile([P, 1], F32, name="warm_out")
        nc.scalar.copy(out=warm_out[:], in_=warm_in[:])
        ident = const.tile([P, P], F32, name="ident")
        make_identity(nc, ident[:])
        bias_bc = const.tile([P, K], BF16, name="bias_bc")

        raws = {}

        def load_w(s, pieces):
            v, u = s // 4, s % 4
            raw = wpool.tile([P, 4, K], BF16, tag="raw", bufs=RAW_BUFS, name="raw%d" % s)
            step = K // pieces
            for i in range(pieces):
                nc.sync.dma_start(
                    out=raw[:, :, i * step : (i + 1) * step], in_=w_view[4 * u + v][:, :, i * step : (i + 1) * step]
                )
            raws[s] = raw

        xraw = {}

        def load_x(v):
            xr = hpool.tile([P, 4 * C], BF16, tag="a01", bufs=4, name="xraw%d" % v)
            nc.sync.dma_start(out=xr[:].rearrange("p (u c) -> p u c", u=4), in_=x_view[v])
            xraw[v] = xr

        load_w(0, 2)
        load_x(0)
        load_x(1)
        load_w(1, 1)
        load_x(2)
        load_x(3)
        load_w(2, 1)
        load_w(3, 1)
        nc.sync.dma_start(out=bias_bc[:], in_=bias.rearrange("a b c k -> (a b c k)").partition_broadcast(P))
        for s in range(4, 8):
            load_w(s, 1)

        xg = {}
        xc = {}
        xs = {}

        def x_transpose(v):
            xw = xraw[v][:].bitcast(F32).rearrange("p (u w h) -> p u h w", u=4, h=2)
            g_t = xpool.tile([P, 4 * P * 4], BF16, tag="xg", bufs=ZT_BUFS, name="xg%d" % v, align_bytes=64)
            g_w = g_t[:].bitcast(F32).rearrange("p (u m h) -> p u m h", u=4, h=2)
            for g in range(2):
                xt = bank(2 * v + g, "xt%d_%d" % (v, g))
                xt4 = xt[:].rearrange("p (u h m) -> p u h m", u=2, h=2)
                for u2 in range(2):
                    for h in range(2):
                        nc.tensor.transpose(xt4[:, u2, h, :], xw[:, 2 * g + u2, h, :], ident[:])
                nc.scalar.copy(
                    out=g_w[:, 2 * g : 2 * g + 2, :, :],
                    in_=xt[:].rearrange("p (u h m) -> p u m h", u=2, h=2),
                )
            xg[v] = g_t

        def x_quantise(v):
            xcv = xpool.tile([P, 2 * 4 * P], U32, name="xc%d" % v, align_bytes=64)
            xsv = xpool.tile([P, 2 * 4 * P], U8, name="xs%d" % v, align_bytes=64)
            xn = xpool.tile([P, 4 * P * 4], BF16, tag="xn", bufs=1, name="xn%d" % v, align_bytes=64)
            nc.vector.tensor_scalar_mul(out=xn[:], in0=xg[v][:], scalar1=-1.0)
            nc.vector.quantize_mx(out=xcv[:, 0:H].bitcast(FP8X4), scales=xsv[:, 0:H], in_=xg[v][:])
            nc.vector.quantize_mx(out=xcv[:, H : 2 * H].bitcast(FP8X4), scales=xsv[:, H : 2 * H], in_=xn[:])
            xc[v] = xcv
            xs[v] = xsv

        grps = {}
        wcs = {}
        wss = {}

        def regroup(n):
            s, k0, w, cut = units[n]
            raw = raws[s]
            grp = wpool.tile([P, w, 4], BF16, tag="grp", bufs=GRP_BUFS, name="grp%d" % n, align_bytes=64)
            nc.scalar.copy(
                out=grp[:, 0:cut, :].rearrange("p (c i) t -> p c t i", i=8),
                in_=raw[:, :, k0 : k0 + cut].rearrange("p t (c i) -> p c t i", i=8),
            )
            if cut < w:
                nc.vector.tensor_copy(
                    out=grp[:, cut:w, :].rearrange("p (c i) t -> p c t i", i=8),
                    in_=raw[:, :, k0 + cut : k0 + w].rearrange("p t (c i) -> p c t i", i=8),
                )
            grps[n] = grp

        def quantise(n):
            s, k0, w, cut = units[n]
            if n < 8:
                wc = wpool.tile([P, w], U32, tag="wc", bufs=CODE_BUFS, name="wc%d" % n, align_bytes=64)
                ws = wpool.tile([P, w], U8, tag="ws", bufs=CODE_BUFS, name="ws%d" % n, align_bytes=64)
            else:
                wc = wpool.tile([P, w], U32, tag="wci", bufs=ITEM_CODE_BUFS, name="wc%d" % n, align_bytes=64)
                ws = wpool.tile([P, w], U8, tag="wsi", bufs=ITEM_CODE_BUFS, name="ws%d" % n, align_bytes=64)
            nc.vector.quantize_mx(
                out=wc[:].bitcast(FP8X4), scales=ws[:], in_=grps[n][:].rearrange("p w j -> p (w j)")
            )
            wcs[n] = wc
            wss[n] = ws

        acc = {}

        def mx_pass(b, n, c0, width, neg, start, stop):
            s = units[n][0]
            v, u = s // 4, s % 4
            o = ((4 if neg else 0) + u) * P
            nc.tensor.matmul_mx(
                out=acc[b][:, 0:width],
                lhsT=xc[v][:, o : o + P].bitcast(FP8X4),
                lhsT_scale=xs[v][:, o : o + P],
                rhs=wcs[n][:, c0 : c0 + width].bitcast(FP8X4),
                rhs_scale=wss[n][:, c0 : c0 + width],
                start=start,
                stop=stop,
            )

        def passes_of(n):
            s, k0, w, cut = units[n]
            v, u = s // 4, s % 4
            res = []
            if v < 2:
                for h in range(2):
                    for p in range(4):
                        res.append((4 * h + p, h * H, H, sign_neg(p, u), u == 0, u == 3))
            else:
                for p in range(4):
                    for q0 in range(2):
                        neg = sign_neg(p, u) != (v == 3 and q0 == 1)
                        res.append((2 * p + q0, 0, w, neg, s == 8, s == 15))
            return res

        def pass_slot(n, b):
            return n + 1 + (LAGS1[b] if n < 8 else LAGS[b])

        def first_slot(n, b):
            return max(pass_slot(n, b), pass_slot(n - 1, b) + 1)

        todo = []
        r0 = {}
        a01 = {}

        def evac_r0(b):
            h = b // 4
            r = hpool.tile([P, H], F32, tag="r0", bufs=8, name="r0_%d" % b)
            nc.vector.scalar_tensor_tensor(
                out=r[:], in0=acc[b][:], scalar=SCALE, in1=bias_bc[:, h * H : (h + 1) * H],
                op0=ALU.mult, op1=ALU.add,
            )
            r0[b] = r

        def evac_a(b):
            h, p = b // 4, b % 4
            if h == 0:
                a01[p] = hpool.tile([P, 2, K], F32, tag="a01", bufs=4, name="a01_%d" % p)
            for q0 in range(2):
                nc.vector.scalar_tensor_tensor(
                    out=a01[p][:, q0, h * H : (h + 1) * H], in0=acc[b][:], scalar=(-SCALE if q0 else SCALE),
                    in1=r0[b][:], op0=ALU.mult, op1=ALU.add,
                )

        def evac_z(c, b):
            k0, w = CHUNKS[c]
            p, q0 = b // 2, b % 2
            zt = xpool.tile([P, 2, w], F32, tag="xg", bufs=ZT_BUFS, name="zt%d_%d" % (c, b), align_bytes=64)
            for q1 in range(2):
                nc.vector.scalar_tensor_tensor(
                    out=zt[:, q1, :], in0=acc[b][:, 0:w], scalar=(-SCALE if q1 else SCALE),
                    in1=a01[p][:, q0, k0 : k0 + w], op0=ALU.mult, op1=ALU.add,
                )
            for q1 in range(2):
                queue = nc.scalar if (c == len(CHUNKS) - 1 and q1 == 1) else nc.sync
                queue.dma_start(out=out_view[p, 2 * q1 + q0][:, :, k0 : k0 + w], in_=zt[:, q1, :])

        evac_at = {}
        for b in range(8):
            jobs = [(first_slot(4, b), 0, 0), (first_slot(8, b), 1, 0)]
            for c in range(len(CHUNKS)):
                jobs.append((first_slot(16 + 8 * c, b), 2, c))
            for when, kind, c in jobs:
                evac_at[when] = evac_at.get(when, []) + [(kind, c, b)]

        for slot in range(n_units + max(LAGS) + 2):
            if slot < n_units:
                regroup(slot)
                if slot < 8:
                    load_w(slot + 8, 1)
            if slot == 0:
                x_transpose(0)
                x_transpose(1)
            if slot == 1:
                x_transpose(2)
                x_transpose(3)
            if slot in X_SLOT:
                x_quantise(X_SLOT[slot])
            if 1 <= slot <= n_units:
                quantise(slot - 1)
                todo.extend([(slot - 1, e) for e in passes_of(slot - 1)])
            for kind, c, b in evac_at.get(slot, []):
                if kind == 0:
                    evac_r0(b)
                elif kind == 1:
                    evac_a(b)
                else:
                    evac_z(c, b)
            now = []
            later = []
            held = set()
            for n, e in todo:
                b, start = e[0], e[4]
                when = first_slot(n, b) if start else pass_slot(n, b)
                if when > slot or b in held:
                    later.append((n, e))
                    held.add(b)
                else:
                    now.append((n, e))
            for n, e in sorted(now, key=lambda t: (t[1][4], t[0], t[1][0])):
                b, c0, width, neg, start, stop = e
                if start:
                    acc[b] = bank(b, "acc%d_%d" % (n, b))
                mx_pass(b, n, c0, width, neg, start, stop)
            todo = later
